import numpy as np
import ml_dtypes


def mxq(x, axis, fmt="e4m3"):
    dtype, down = {"e4m3": (ml_dtypes.float8_e4m3fn, 7), "e5m2": (ml_dtypes.float8_e5m2, 14)}[fmt]
    v = np.moveaxis(np.asarray(x, np.float32).astype(ml_dtypes.bfloat16).astype(np.float64), axis, -1)
    blocks = v.reshape(v.shape[:-1] + (-1, 32))
    amax = np.abs(blocks).max(-1, keepdims=True)
    byte = np.maximum(np.where(amax > 0, np.frexp(amax)[1] - 1 + 127, 0) - down, 1)
    scale = np.exp2(byte - 127.0)
    codes = (blocks / scale).astype(np.float32).astype(dtype).astype(np.float64)
    return np.moveaxis((codes * scale).reshape(v.shape), -1, axis)


WIDE = False


def mx_kscale(k):
    if not WIDE:
        return np.ones(k)
    levels = np.array([20, -20, 10, -10, 0])
    a = np.random.permutation(np.resize(levels, k // 512 * 4)).reshape(k // 512, 4)
    idx = np.arange(k)
    return np.exp2(a[idx // 512, idx % 128 // 32])


BF16 = ml_dtypes.bfloat16


def bf(x):
    return np.asarray(x, np.float32).astype(BF16)


def f64(x):
    return np.asarray(x).astype(np.float64)


B, S, D, H = 2, 256, 512, 4
DH = D // H


def softmax(v, axis):
    e = np.exp(v - v.max(axis, keepdims=True))
    return e / e.sum(axis, keepdims=True)


def setup_inputs():
    u = mx_kscale(D)
    q_soft = softmax(np.random.standard_normal((B, H, S, DH)) * 1.5, -1)
    kv = np.random.standard_normal((B, H, DH, DH)) * 6.0 * np.sqrt(S) / DH
    W_O = np.random.standard_normal((D, H * DH)) * 2.0 / np.sqrt(D) / u[:, None]
    g = np.random.standard_normal((B, S, D)) * np.exp2(np.random.randint(-12, 1, (B, S, 1))) * u
    return {"q_soft": bf(q_soft), "kv": bf(kv), "W_O": bf(W_O), "grad_out": bf(g)}


def reference(q_soft, kv, W_O, grad_out):
    gy = mxq(f64(grad_out), 2, "e5m2") @ mxq(f64(W_O), 0, "e4m3")
    gbt = gy.reshape(B, H, S, DH)
    return gbt @ f64(kv).transpose(0, 1, 3, 2)

@@ -1,0 +1,148 @@
+from contextlib import ExitStack
+
+import concourse.mybir as mybir
+from concourse.masks import make_identity
+
+F32 = mybir.dt.float32
+BF16 = mybir.dt.bfloat16
+U32 = mybir.dt.uint32
+U8 = mybir.dt.uint8
+E4M3_X4 = mybir.dt.float8_e4m3fn_x4
+E5M2_X4 = mybir.dt.float8_e5m2_x4
+
+P = 128
+PACK = 4
+BATCH, HEADS_PER_BATCH, SEQ, HEAD_DIM = 2, 4, 256, 128
+FEATURES = HEADS_PER_BATCH * HEAD_DIM
+TOKENS = BATCH * SEQ
+HEADS = BATCH * HEADS_PER_BATCH
+HEAD_TOKENS = TOKENS // HEADS
+PASSES = FEATURES // HEAD_DIM
+TOKEN_SETS = TOKENS // P
+
+FLOPS = 2 * TOKENS * FEATURES * FEATURES + 2 * HEADS * SEQ * HEAD_DIM * HEAD_DIM
+BYTES = 2 * (HEADS * HEAD_DIM * HEAD_DIM + FEATURES * FEATURES + TOKENS * FEATURES) + 4 * HEADS * SEQ * HEAD_DIM
+
+
+def tile_mhla2_pb_s_kernel(tc, q_soft, kv, W_O, grad_out, out):
+    nc = tc.nc
+    with ExitStack() as ctx:
+        sbuf = ctx.enter_context(tc.tile_pool(name="sbuf", bufs=1))
+        psum_gy = ctx.enter_context(tc.psum_pool(name="psum_gy", bufs=PASSES))
+        psum_work = ctx.enter_context(tc.psum_pool(name="psum_work", bufs=4))
+
+        ident_f32 = sbuf.tile([P, P], F32)
+        make_identity(nc, ident_f32[:])
+        ident_bf16 = sbuf.tile([P, P], BF16)
+        make_identity(nc, ident_bf16[:])
+
+        w_raw = sbuf.tile([P, PACK, FEATURES], BF16)
+        nc.sync.dma_start(
+            out=w_raw[:].rearrange("q (u e) i -> q u (e i)", u=2),
+            in_=W_O.rearrange("(u q e) i -> q u (e i)", u=2, e=2),
+        )
+        g_raw = sbuf.tile([P, TOKEN_SETS * FEATURES], BF16)
+        g_rows = grad_out.rearrange("b s o -> (b s) o").rearrange("(p n) o -> p (n o)", n=TOKEN_SETS)
+        half_row = TOKEN_SETS * FEATURES // 2
+        for half in range(2):
+            cols = slice(half * half_row, (half + 1) * half_row)
+            nc.sync.dma_start(out=g_raw[:, cols], in_=g_rows[:, cols])
+        kv_raw = sbuf.tile([P, BATCH, PACK, HEAD_DIM], BF16)
+        nc.sync.dma_start(
+            out=kv_raw[:].rearrange("p b r e -> p b (r e)"),
+            in_=kv.rearrange("b h d e -> b (h d) e").rearrange("b (p r) e -> p b (r e)", r=PACK),
+        )
+
+        w_grouped = sbuf.tile([P, FEATURES, PACK], BF16, align_bytes=64)
+        nc.vector.tensor_copy(
+            out=w_grouped[:].rearrange("q (c i) t -> q c t i", i=4),
+            in_=w_raw[:].rearrange("q t (c i) -> q c t i", i=4),
+        )
+        w_codes = sbuf.tile([P, FEATURES], U32, align_bytes=64)
+        w_scales = sbuf.tile([P, FEATURES], U8, align_bytes=64)
+        nc.vector.quantize_mx(
+            out=w_codes[:].bitcast(E4M3_X4),
+            scales=w_scales[:],
+            in_=w_grouped[:].rearrange("q i t -> q (i t)"),
+        )
+
+        g_words = g_raw[:].bitcast(F32)
+        g_grouped = sbuf.tile([P, TOKENS * PACK], BF16, align_bytes=64)
+        g_grouped_words = g_grouped[:].bitcast(F32).rearrange("q (n p u) -> q n p u", n=TOKEN_SETS, u=2)
+        g_codes = sbuf.tile([P, TOKENS], U32, align_bytes=64)
+        g_scales = sbuf.tile([P, TOKENS], U8, align_bytes=64)
+        words_per_token = FEATURES // 2
+        for half in range(2):
+            g_t = psum_work.tile([P, 2, 2, P], F32, tag="work", name="g_t")
+            for m in range(2):
+                for u in range(2):
+                    first = (2 * half + m) * words_per_token + u * P
+                    nc.tensor.transpose(g_t[:, m, u, :], g_words[:, first : first + P], ident_f32[:])
+            nc.scalar.copy(
+                out=g_grouped_words[:, 2 * half : 2 * half + 2, :, :],
+                in_=g_t[:].rearrange("q m u p -> q m p u"),
+            )
+            tokens = slice(half * TOKENS // 2, (half + 1) * TOKENS // 2)
+            nc.vector.quantize_mx(
+                out=g_codes[:, tokens].bitcast(E5M2_X4),
+                scales=g_scales[:, tokens],
+                in_=g_grouped[:, half * TOKENS * 2 : (half + 1) * TOKENS * 2],
+            )
+
+        kv_t = sbuf.tile([P, HEADS, HEAD_DIM], F32)
+        for b in range(BATCH):
+            kv_ps = psum_work.tile([P, PACK, P], BF16, tag="work", name="kv_ps")
+            for r in range(PACK):
+                nc.tensor.transpose(kv_ps[:, r, :], kv_raw[:, b, r, :], ident_bf16[:])
+            copy_out = nc.scalar.copy if b == 0 else nc.vector.tensor_copy
+            copy_out(
+                out=kv_t[:, HEADS_PER_BATCH * b : HEADS_PER_BATCH * (b + 1), :].rearrange(
+                    "e h (c r) -> e (h c) r", r=PACK
+                ),
+                in_=kv_ps[:].rearrange("e r p -> e p r"),
+            )
+
+        gy_ps = [psum_gy.tile([P, TOKENS], F32, tag="gy", name="gy_ps%d" % j) for j in range(PASSES)]
+        for j in (0, 2, 1, 3):
+            nc.tensor.matmul_mx(
+                out=gy_ps[j][:],
+                lhsT=w_codes[:, j * P : (j + 1) * P].bitcast(E4M3_X4),
+                lhsT_scale=w_scales[:, j * P : (j + 1) * P],
+                rhs=g_codes[:].bitcast(E5M2_X4),
+                rhs_scale=g_scales[:],
+                start=True,
+                stop=True,
+            )
+
+        gy_sb = sbuf.tile([P, HEADS, 2, 2, HEAD_TOKENS], F32)
+        for b in range(BATCH):
+            heads = slice(HEADS_PER_BATCH * b, HEADS_PER_BATCH * (b + 1))
+            for jj in range(2):
+                for jp in range(2):
+                    copy_out = nc.vector.tensor_copy if jp == 0 else nc.scalar.copy
+                    copy_out(
+                        out=gy_sb[:, heads, jj, jp, :].rearrange("e h (c n) -> e h c n", n=TOKEN_SETS),
+                        in_=gy_ps[2 * jp + jj][:].rearrange("e (n h c) -> e h c n", n=TOKEN_SETS, h=HEADS)[
+                            :, heads, :, :
+                        ],
+                    )
+
+        out_rows = out.rearrange("b h (rr jp jj) d -> jp rr (b h) (jj d)", jp=2, jj=2)
+        result = sbuf.tile([P, HEADS, 2 * HEAD_DIM], F32)
+        for head in range(HEADS):
+            out_ps = psum_work.tile([P, 2, HEAD_DIM], F32, tag="work", name="out_ps")
+            for jj in range(2):
+                nc.tensor.matmul(
+                    out=out_ps[:, jj, :],
+                    lhsT=gy_sb[:, head, jj, :, :].rearrange("e jp rr -> e (jp rr)"),
+                    rhs=kv_t[:, head, :],
+                    start=True,
+                    stop=True,
+                )
+            copy_out = nc.vector.tensor_copy if head % 2 == 0 else nc.scalar.copy
+            copy_out(out=result[:, head, :], in_=out_ps[:].rearrange("s jj d -> s (jj d)"))
+            if head % 2 == 1:
+                pair = slice(head - 1, head + 1)
+                for jp in range(2):
+                    rows = slice(jp * HEAD_TOKENS, (jp + 1) * HEAD_TOKENS)
+                    nc.sync.dma_start(out=out_rows[jp, :, pair, :], in_=result[rows, pair, :])

@@ -27,6 +27,7 @@ BYTES = 2 * (HEADS * HEAD_DIM * HEAD_DIM + FEATURES * FEATURES + TOKENS * FEATUR
 def tile_mhla2_pb_s_kernel(tc, q_soft, kv, W_O, grad_out, out):
     nc = tc.nc
     with ExitStack() as ctx:
+        ctx.enter_context(tc.manual_schedule())
         sbuf = ctx.enter_context(tc.tile_pool(name="sbuf", bufs=1))
         psum_gy = ctx.enter_context(tc.psum_pool(name="psum_gy", bufs=PASSES))
         psum_work = ctx.enter_context(tc.psum_pool(name="psum_work", bufs=4))
@@ -43,9 +44,8 @@ def tile_mhla2_pb_s_kernel(tc, q_soft, kv, W_O, grad_out, out):
         )
         g_raw = sbuf.tile([P, TOKEN_SETS * FEATURES], BF16)
         g_rows = grad_out.rearrange("b s o -> (b s) o").rearrange("(p n) o -> p (n o)", n=TOKEN_SETS)
-        half_row = TOKEN_SETS * FEATURES // 2
-        for half in range(2):
-            cols = slice(half * half_row, (half + 1) * half_row)
+        for n in range(TOKEN_SETS):
+            cols = slice(n * FEATURES, (n + 1) * FEATURES)
             nc.sync.dma_start(out=g_raw[:, cols], in_=g_rows[:, cols])
         kv_raw = sbuf.tile([P, BATCH, PACK, HEAD_DIM], BF16)
         nc.sync.dma_start(
@@ -54,10 +54,11 @@ def tile_mhla2_pb_s_kernel(tc, q_soft, kv, W_O, grad_out, out):
         )
 
         w_grouped = sbuf.tile([P, FEATURES, PACK], BF16, align_bytes=64)
-        nc.vector.tensor_copy(
-            out=w_grouped[:].rearrange("q (c i) t -> q c t i", i=4),
-            in_=w_raw[:].rearrange("q t (c i) -> q c t i", i=4),
-        )
+        for copy, cols in ((nc.scalar.copy, slice(3 * P, 4 * P)), (nc.vector.tensor_copy, slice(0, 3 * P))):
+            copy(
+                out=w_grouped[:, cols, :].rearrange("q (c i) t -> q c t i", i=4),
+                in_=w_raw[:, :, cols].rearrange("q t (c i) -> q c t i", i=4),
+            )
         w_codes = sbuf.tile([P, FEATURES], U32, align_bytes=64)
         w_scales = sbuf.tile([P, FEATURES], U8, align_bytes=64)
         nc.vector.quantize_mx(
@@ -72,21 +73,16 @@ def tile_mhla2_pb_s_kernel(tc, q_soft, kv, W_O, grad_out, out):
         g_codes = sbuf.tile([P, TOKENS], U32, align_bytes=64)
         g_scales = sbuf.tile([P, TOKENS], U8, align_bytes=64)
         words_per_token = FEATURES // 2
-        for half in range(2):
-            g_t = psum_work.tile([P, 2, 2, P], F32, tag="work", name="g_t")
-            for m in range(2):
-                for u in range(2):
-                    first = (2 * half + m) * words_per_token + u * P
-                    nc.tensor.transpose(g_t[:, m, u, :], g_words[:, first : first + P], ident_f32[:])
-            nc.scalar.copy(
-                out=g_grouped_words[:, 2 * half : 2 * half + 2, :, :],
-                in_=g_t[:].rearrange("q m u p -> q m p u"),
-            )
-            tokens = slice(half * TOKENS // 2, (half + 1) * TOKENS // 2)
+        for n in range(TOKEN_SETS):
+            g_t = psum_work.tile([P, 2, P], F32, tag="work", name="g_t")
+            for u in range(2):
+                first = n * words_per_token + u * P
+                nc.tensor.transpose(g_t[:, u, :], g_words[:, first : first + P], ident_f32[:])
+            nc.scalar.copy(out=g_grouped_words[:, n, :, :], in_=g_t[:].rearrange("q u p -> q p u"))
             nc.vector.quantize_mx(
-                out=g_codes[:, tokens].bitcast(E5M2_X4),
-                scales=g_scales[:, tokens],
-                in_=g_grouped[:, half * TOKENS * 2 : (half + 1) * TOKENS * 2],
+                out=g_codes[:, n * P : (n + 1) * P].bitcast(E5M2_X4),
+                scales=g_scales[:, n * P : (n + 1) * P],
+                in_=g_grouped[:, n * P * PACK : (n + 1) * P * PACK],
             )
 
         kv_t = sbuf.tile([P, HEADS, HEAD_DIM], F32)
@@ -94,8 +90,8 @@ def tile_mhla2_pb_s_kernel(tc, q_soft, kv, W_O, grad_out, out):
             kv_ps = psum_work.tile([P, PACK, P], BF16, tag="work", name="kv_ps")
             for r in range(PACK):
                 nc.tensor.transpose(kv_ps[:, r, :], kv_raw[:, b, r, :], ident_bf16[:])
-            copy_out = nc.scalar.copy if b == 0 else nc.vector.tensor_copy
-            copy_out(
+            copy = nc.scalar.copy if b == 0 else nc.vector.tensor_copy
+            copy(
                 out=kv_t[:, HEADS_PER_BATCH * b : HEADS_PER_BATCH * (b + 1), :].rearrange(
                     "e h (c r) -> e (h c) r", r=PACK
                 ),
@@ -119,8 +115,8 @@ def tile_mhla2_pb_s_kernel(tc, q_soft, kv, W_O, grad_out, out):
             heads = slice(HEADS_PER_BATCH * b, HEADS_PER_BATCH * (b + 1))
             for jj in range(2):
                 for jp in range(2):
-                    copy_out = nc.vector.tensor_copy if jp == 0 else nc.scalar.copy
-                    copy_out(
+                    copy = nc.vector.tensor_copy if jp == 0 else nc.scalar.copy
+                    copy(
                         out=gy_sb[:, heads, jj, jp, :].rearrange("e h (c n) -> e h c n", n=TOKEN_SETS),
                         in_=gy_ps[2 * jp + jj][:].rearrange("e (n h c) -> e h c n", n=TOKEN_SETS, h=HEADS)[
                             :, heads, :, :
@@ -129,20 +125,23 @@ def tile_mhla2_pb_s_kernel(tc, q_soft, kv, W_O, grad_out, out):
 
         out_rows = out.rearrange("b h (rr jp jj) d -> jp rr (b h) (jj d)", jp=2, jj=2)
         result = sbuf.tile([P, HEADS, 2 * HEAD_DIM], F32)
-        for head in range(HEADS):
-            out_ps = psum_work.tile([P, 2, HEAD_DIM], F32, tag="work", name="out_ps")
+        for first_head in range(0, HEADS, 2):
+            pair = (first_head, first_head + 1)
+            out_ps = [psum_work.tile([P, 2, HEAD_DIM], F32, tag="work", name="out_ps%d" % head) for head in pair]
             for jj in range(2):
-                nc.tensor.matmul(
-                    out=out_ps[:, jj, :],
-                    lhsT=gy_sb[:, head, jj, :, :].rearrange("e jp rr -> e (jp rr)"),
-                    rhs=kv_t[:, head, :],
-                    start=True,
-                    stop=True,
+                for k, head in enumerate(pair):
+                    nc.tensor.matmul(
+                        out=out_ps[k][:, jj, :],
+                        lhsT=gy_sb[:, head, jj, :, :].rearrange("e jp rr -> e (jp rr)"),
+                        rhs=kv_t[:, head, :],
+                        start=True,
+                        stop=True,
+                    )
+            nc.vector.tensor_copy(out=result[:, pair[0], :], in_=out_ps[0][:].rearrange("s jj d -> s (jj d)"))
+            nc.scalar.copy(out=result[:, pair[1], :], in_=out_ps[1][:].rearrange("s jj d -> s (jj d)"))
+            for jp in range(2):
+                rows = slice(jp * HEAD_TOKENS, (jp + 1) * HEAD_TOKENS)
+                nc.sync.dma_start(
+                    out=out_rows[jp, :, first_head : first_head + 2, :],
+                    in_=result[rows, first_head : first_head + 2, :],
                 )
-            copy_out = nc.vector.tensor_copy if head % 2 == 0 else nc.scalar.copy
-            copy_out(out=result[:, head, :], in_=out_ps[:].rearrange("s jj d -> s (jj d)"))
-            if head % 2 == 1:
-                pair = slice(head - 1, head + 1)
-                for jp in range(2):
-                    rows = slice(jp * HEAD_TOKENS, (jp + 1) * HEAD_TOKENS)
-                    nc.sync.dma_start(out=out_rows[jp, :, pair, :], in_=result[rows, pair, :])

@@ -7,6 +7,7 @@ F32 = mybir.dt.float32
 BF16 = mybir.dt.bfloat16
 U32 = mybir.dt.uint32
 U8 = mybir.dt.uint8
+I32 = mybir.dt.int32
 E4M3_X4 = mybir.dt.float8_e4m3fn_x4
 E5M2_X4 = mybir.dt.float8_e5m2_x4
 
@@ -19,6 +20,8 @@ HEADS = BATCH * HEADS_PER_BATCH
 HEAD_TOKENS = TOKENS // HEADS
 PASSES = FEATURES // HEAD_DIM
 TOKEN_SETS = TOKENS // P
+WARM_FIRST = 4
+WARM_LAST = 1
 
 FLOPS = 2 * TOKENS * FEATURES * FEATURES + 2 * HEADS * SEQ * HEAD_DIM * HEAD_DIM
 BYTES = 2 * (HEADS * HEAD_DIM * HEAD_DIM + FEATURES * FEATURES + TOKENS * FEATURES) + 4 * HEADS * SEQ * HEAD_DIM
@@ -32,10 +35,41 @@ def tile_mhla2_pb_s_kernel(tc, q_soft, kv, W_O, grad_out, out):
         psum_gy = ctx.enter_context(tc.psum_pool(name="psum_gy", bufs=PASSES))
         psum_work = ctx.enter_context(tc.psum_pool(name="psum_work", bufs=4))
 
+        gy_ps = [psum_gy.tile([P, TOKENS], F32, tag="gy", name="gy_ps%d" % j) for j in range(PASSES)]
+        zeros = sbuf.tile([P, P * PACK], BF16, align_bytes=64)
+        nc.vector.memset(zeros[:].bitcast(I32), 0)
+        zero_w_codes = sbuf.tile([P, P], U32, align_bytes=64)
+        zero_w_scales = sbuf.tile([P, P], U8, align_bytes=64)
+        nc.vector.quantize_mx(out=zero_w_codes[:].bitcast(E4M3_X4), scales=zero_w_scales[:], in_=zeros[:])
+        zero_g_codes = sbuf.tile([P, TOKENS], U32, align_bytes=64)
+        zero_g_scales = sbuf.tile([P, TOKENS], U8, align_bytes=64)
+        for n in range(TOKEN_SETS):
+            nc.vector.quantize_mx(
+                out=zero_g_codes[:, n * P : (n + 1) * P].bitcast(E5M2_X4),
+                scales=zero_g_scales[:, n * P : (n + 1) * P],
+                in_=zeros[:],
+            )
+
+        def warm_passes(count):
+            for i in range(count):
+                nc.tensor.matmul_mx(
+                    out=gy_ps[PASSES - 1][:],
+                    lhsT=zero_w_codes[:].bitcast(E4M3_X4),
+                    lhsT_scale=zero_w_scales[:],
+                    rhs=zero_g_codes[:].bitcast(E5M2_X4),
+                    rhs_scale=zero_g_scales[:],
+                    start=True,
+                    stop=True,
+                )
+
+        warm_passes(WARM_FIRST)
+
         ident_f32 = sbuf.tile([P, P], F32)
-        make_identity(nc, ident_f32[:])
+        nc.vector.memset(ident_f32[:], 0.0)
+        make_identity(nc, ident_f32[:], nomemset=True)
         ident_bf16 = sbuf.tile([P, P], BF16)
-        make_identity(nc, ident_bf16[:])
+        nc.vector.memset(ident_bf16[:], 0.0)
+        make_identity(nc, ident_bf16[:], nomemset=True)
 
         w_raw = sbuf.tile([P, PACK, FEATURES], BF16)
         nc.sync.dma_start(
@@ -85,6 +119,8 @@ def tile_mhla2_pb_s_kernel(tc, q_soft, kv, W_O, grad_out, out):
                 in_=g_grouped[:, n * P * PACK : (n + 1) * P * PACK],
             )
 
+        warm_passes(WARM_LAST)
+
         kv_t = sbuf.tile([P, HEADS, HEAD_DIM], F32)
         for b in range(BATCH):
             kv_ps = psum_work.tile([P, PACK, P], BF16, tag="work", name="kv_ps")
@@ -98,7 +134,6 @@ def tile_mhla2_pb_s_kernel(tc, q_soft, kv, W_O, grad_out, out):
                 in_=kv_ps[:].rearrange("e r p -> e p r"),
             )
 
-        gy_ps = [psum_gy.tile([P, TOKENS], F32, tag="gy", name="gy_ps%d" % j) for j in range(PASSES)]
         for j in (0, 2, 1, 3):
             nc.tensor.matmul_mx(
                 out=gy_ps[j][:],

@@ -20,8 +20,8 @@ HEADS = BATCH * HEADS_PER_BATCH
 HEAD_TOKENS = TOKENS // HEADS
 PASSES = FEATURES // HEAD_DIM
 TOKEN_SETS = TOKENS // P
-WARM_FIRST = 4
-WARM_LAST = 1
+WARM_FIRST = 3
+WARM_LAST = 2
 
 FLOPS = 2 * TOKENS * FEATURES * FEATURES + 2 * HEADS * SEQ * HEAD_DIM * HEAD_DIM
 BYTES = 2 * (HEADS * HEAD_DIM * HEAD_DIM + FEATURES * FEATURES + TOKENS * FEATURES) + 4 * HEADS * SEQ * HEAD_DIM
@@ -77,10 +77,9 @@ def tile_mhla2_pb_s_kernel(tc, q_soft, kv, W_O, grad_out, out):
             in_=W_O.rearrange("(u q e) i -> q u (e i)", u=2, e=2),
         )
         g_raw = sbuf.tile([P, TOKEN_SETS * FEATURES], BF16)
-        g_rows = grad_out.rearrange("b s o -> (b s) o").rearrange("(p n) o -> p (n o)", n=TOKEN_SETS)
+        g_rows = grad_out.rearrange("b s o -> (b s) o").rearrange("(n p) o -> n p o", p=P)
         for n in range(TOKEN_SETS):
-            cols = slice(n * FEATURES, (n + 1) * FEATURES)
-            nc.sync.dma_start(out=g_raw[:, cols], in_=g_rows[:, cols])
+            nc.sync.dma_start(out=g_raw[:, n * FEATURES : (n + 1) * FEATURES], in_=g_rows[n])
         kv_raw = sbuf.tile([P, BATCH, PACK, HEAD_DIM], BF16)
         nc.sync.dma_start(
             out=kv_raw[:].rearrange("p b r e -> p b (r e)"),
@@ -152,10 +151,8 @@ def tile_mhla2_pb_s_kernel(tc, q_soft, kv, W_O, grad_out, out):
                 for jp in range(2):
                     copy = nc.vector.tensor_copy if jp == 0 else nc.scalar.copy
                     copy(
-                        out=gy_sb[:, heads, jj, jp, :].rearrange("e h (c n) -> e h c n", n=TOKEN_SETS),
-                        in_=gy_ps[2 * jp + jj][:].rearrange("e (n h c) -> e h c n", n=TOKEN_SETS, h=HEADS)[
-                            :, heads, :, :
-                        ],
+                        out=gy_sb[:, heads, jj, jp, :],
+                        in_=gy_ps[2 * jp + jj][:].rearrange("e (h rr) -> e h rr", h=HEADS)[:, heads, :],
                     )
 
         out_rows = out.rearrange("b h (rr jp jj) d -> jp rr (b h) (jj d)", jp=2, jj=2)
@@ -174,9 +171,7 @@ def tile_mhla2_pb_s_kernel(tc, q_soft, kv, W_O, grad_out, out):
                     )
             nc.vector.tensor_copy(out=result[:, pair[0], :], in_=out_ps[0][:].rearrange("s jj d -> s (jj d)"))
             nc.scalar.copy(out=result[:, pair[1], :], in_=out_ps[1][:].rearrange("s jj d -> s (jj d)"))
-            for jp in range(2):
-                rows = slice(jp * HEAD_TOKENS, (jp + 1) * HEAD_TOKENS)
-                nc.sync.dma_start(
-                    out=out_rows[jp, :, first_head : first_head + 2, :],
-                    in_=result[rows, first_head : first_head + 2, :],
-                )
+            for head in pair:
+                for jp in range(2):
+                    rows = slice(jp * HEAD_TOKENS, (jp + 1) * HEAD_TOKENS)
+                    nc.sync.dma_start(out=out_rows[jp, :, head, :], in_=result[rows, head, :])

@@ -171,7 +171,7 @@ def tile_mhla2_pb_s_kernel(tc, q_soft, kv, W_O, grad_out, out):
                     )
             nc.vector.tensor_copy(out=result[:, pair[0], :], in_=out_ps[0][:].rearrange("s jj d -> s (jj d)"))
             nc.scalar.copy(out=result[:, pair[1], :], in_=out_ps[1][:].rearrange("s jj d -> s (jj d)"))
-            for head in pair:
+            for queue, head in zip((nc.sync, nc.scalar), pair):
                 for jp in range(2):
                     rows = slice(jp * HEAD_TOKENS, (jp + 1) * HEAD_TOKENS)
-                    nc.sync.dma_start(out=out_rows[jp, :, head, :], in_=result[rows, head, :])
+                    queue.dma_start(out=out_rows[jp, :, head, :], in_=result[rows, head, :])

@@ -121,17 +121,21 @@ def tile_mhla2_pb_s_kernel(tc, q_soft, kv, W_O, grad_out, out):
         warm_passes(WARM_LAST)
 
         kv_t = sbuf.tile([P, HEADS, HEAD_DIM], F32)
+        kv_ps = []
         for b in range(BATCH):
-            kv_ps = psum_work.tile([P, PACK, P], BF16, tag="work", name="kv_ps")
+            kv_ps.append(psum_work.tile([P, PACK, P], BF16, tag="work", name="kv_ps%d" % b))
             for r in range(PACK):
-                nc.tensor.transpose(kv_ps[:, r, :], kv_raw[:, b, r, :], ident_bf16[:])
-            copy = nc.scalar.copy if b == 0 else nc.vector.tensor_copy
+                nc.tensor.transpose(kv_ps[b][:, r, :], kv_raw[:, b, r, :], ident_bf16[:])
+
+        def kv_copy(copy, b):
             copy(
                 out=kv_t[:, HEADS_PER_BATCH * b : HEADS_PER_BATCH * (b + 1), :].rearrange(
                     "e h (c r) -> e (h c) r", r=PACK
                 ),
-                in_=kv_ps[:].rearrange("e r p -> e p r"),
+                in_=kv_ps[b][:].rearrange("e r p -> e p r"),
             )
+
+        kv_copy(nc.scalar.copy, 0)
 
         for j in (0, 2, 1, 3):
             nc.tensor.matmul_mx(
@@ -154,24 +158,38 @@ def tile_mhla2_pb_s_kernel(tc, q_soft, kv, W_O, grad_out, out):
                         out=gy_sb[:, heads, jj, jp, :],
                         in_=gy_ps[2 * jp + jj][:].rearrange("e (h rr) -> e h rr", h=HEADS)[:, heads, :],
                     )
+            if b == 0:
+                kv_copy(nc.vector.tensor_copy, 1)
 
         out_rows = out.rearrange("b h (rr jp jj) d -> jp rr (b h) (jj d)", jp=2, jj=2)
         result = sbuf.tile([P, HEADS, 2 * HEAD_DIM], F32)
         for first_head in range(0, HEADS, 2):
             pair = (first_head, first_head + 1)
-            out_ps = [psum_work.tile([P, 2, HEAD_DIM], F32, tag="work", name="out_ps%d" % head) for head in pair]
+            last = first_head == HEADS - 2
+            if last:
+                halves = [
+                    [psum_gy.tile([P, HEAD_DIM], F32, tag="gy", name="half_ps%d%d" % (k, jj)) for jj in range(2)]
+                    for k in range(2)
+                ]
+            else:
+                out_ps = [psum_work.tile([P, 2, HEAD_DIM], F32, tag="work", name="out_ps%d" % head) for head in pair]
+                halves = [[out_ps[k][:, jj, :] for jj in range(2)] for k in range(2)]
             for jj in range(2):
                 for k, head in enumerate(pair):
                     nc.tensor.matmul(
-                        out=out_ps[k][:, jj, :],
+                        out=halves[k][jj][:] if last else halves[k][jj],
                         lhsT=gy_sb[:, head, jj, :, :].rearrange("e jp rr -> e (jp rr)"),
                         rhs=kv_t[:, head, :],
                         start=True,
                         stop=True,
                     )
-            nc.vector.tensor_copy(out=result[:, pair[0], :], in_=out_ps[0][:].rearrange("s jj d -> s (jj d)"))
-            nc.scalar.copy(out=result[:, pair[1], :], in_=out_ps[1][:].rearrange("s jj d -> s (jj d)"))
-            for queue, head in zip((nc.sync, nc.scalar), pair):
+                    if last:
+                        copy = nc.scalar.copy if k == 0 else nc.vector.tensor_copy
+                        copy(out=result[:, head, jj * HEAD_DIM : (jj + 1) * HEAD_DIM], in_=halves[k][jj][:])
+            if not last:
+                nc.vector.tensor_copy(out=result[:, pair[0], :], in_=out_ps[0][:].rearrange("s jj d -> s (jj d)"))
+                nc.scalar.copy(out=result[:, pair[1], :], in_=out_ps[1][:].rearrange("s jj d -> s (jj d)"))
+            for head in pair:
                 for jp in range(2):
                     rows = slice(jp * HEAD_TOKENS, (jp + 1) * HEAD_TOKENS)
-                    queue.dma_start(out=out_rows[jp, :, head, :], in_=result[rows, head, :])
+                    nc.sync.dma_start(out=out_rows[jp, :, head, :], in_=result[rows, head, :])

@@ -78,8 +78,15 @@ def tile_mhla2_pb_s_kernel(tc, q_soft, kv, W_O, grad_out, out):
         )
         g_raw = sbuf.tile([P, TOKEN_SETS * FEATURES], BF16)
         g_rows = grad_out.rearrange("b s o -> (b s) o").rearrange("(n p) o -> n p o", p=P)
-        for n in range(TOKEN_SETS):
+        for n in range(TOKEN_SETS - 1):
             nc.sync.dma_start(out=g_raw[:, n * FEATURES : (n + 1) * FEATURES], in_=g_rows[n])
+        last_set = TOKEN_SETS - 1
+        for u in range(2):
+            half = slice(u * FEATURES // 2, (u + 1) * FEATURES // 2)
+            nc.sync.dma_start(
+                out=g_raw[:, last_set * FEATURES + u * FEATURES // 2 : last_set * FEATURES + (u + 1) * FEATURES // 2],
+                in_=g_rows[last_set][:, half],
+            )
         kv_raw = sbuf.tile([P, BATCH, PACK, HEAD_DIM], BF16)
         nc.sync.dma_start(
             out=kv_raw[:].rearrange("p b r e -> p b (r e)"),
@@ -149,16 +156,16 @@ def tile_mhla2_pb_s_kernel(tc, q_soft, kv, W_O, grad_out, out):
             )
 
         gy_sb = sbuf.tile([P, HEADS, 2, 2, HEAD_TOKENS], F32)
-        for b in range(BATCH):
-            heads = slice(HEADS_PER_BATCH * b, HEADS_PER_BATCH * (b + 1))
+        for first, count in ((0, 2), (2, 2), (4, 4)):
+            heads = slice(first, first + count)
             for jj in range(2):
                 for jp in range(2):
-                    copy = nc.vector.tensor_copy if jp == 0 else nc.scalar.copy
+                    copy = nc.scalar.copy if jp == 0 else nc.vector.tensor_copy
                     copy(
                         out=gy_sb[:, heads, jj, jp, :],
                         in_=gy_ps[2 * jp + jj][:].rearrange("e (h rr) -> e h rr", h=HEADS)[:, heads, :],
                     )
-            if b == 0:
+            if first == 2:
                 kv_copy(nc.vector.tensor_copy, 1)
 
         out_rows = out.rearrange("b h (rr jp jj) d -> jp rr (b h) (jj d)", jp=2, jj=2)

from contextlib import ExitStack

import concourse.mybir as mybir
from concourse.masks import make_identity

F32 = mybir.dt.float32
BF16 = mybir.dt.bfloat16
U32 = mybir.dt.uint32
U8 = mybir.dt.uint8
I32 = mybir.dt.int32
E4M3_X4 = mybir.dt.float8_e4m3fn_x4
E5M2_X4 = mybir.dt.float8_e5m2_x4

P = 128
PACK = 4
BATCH, HEADS_PER_BATCH, SEQ, HEAD_DIM = 2, 4, 256, 128
FEATURES = HEADS_PER_BATCH * HEAD_DIM
TOKENS = BATCH * SEQ
HEADS = BATCH * HEADS_PER_BATCH
HEAD_TOKENS = TOKENS // HEADS
PASSES = FEATURES // HEAD_DIM
TOKEN_SETS = TOKENS // P
WARM_FIRST = 3
WARM_LAST = 2

FLOPS = 2 * TOKENS * FEATURES * FEATURES + 2 * HEADS * SEQ * HEAD_DIM * HEAD_DIM
BYTES = 2 * (HEADS * HEAD_DIM * HEAD_DIM + FEATURES * FEATURES + TOKENS * FEATURES) + 4 * HEADS * SEQ * HEAD_DIM


def tile_mhla2_pb_s_kernel(tc, q_soft, kv, W_O, grad_out, out):
    nc = tc.nc
    with ExitStack() as ctx:
        ctx.enter_context(tc.manual_schedule())
        sbuf = ctx.enter_context(tc.tile_pool(name="sbuf", bufs=1))
        psum_gy = ctx.enter_context(tc.psum_pool(name="psum_gy", bufs=PASSES))
        psum_work = ctx.enter_context(tc.psum_pool(name="psum_work", bufs=4))

        gy_ps = [psum_gy.tile([P, TOKENS], F32, tag="gy", name="gy_ps%d" % j) for j in range(PASSES)]
        zeros = sbuf.tile([P, P * PACK], BF16, align_bytes=64)
        nc.vector.memset(zeros[:].bitcast(I32), 0)
        zero_w_codes = sbuf.tile([P, P], U32, align_bytes=64)
        zero_w_scales = sbuf.tile([P, P], U8, align_bytes=64)
        nc.vector.quantize_mx(out=zero_w_codes[:].bitcast(E4M3_X4), scales=zero_w_scales[:], in_=zeros[:])
        zero_g_codes = sbuf.tile([P, TOKENS], U32, align_bytes=64)
        zero_g_scales = sbuf.tile([P, TOKENS], U8, align_bytes=64)
        for n in range(TOKEN_SETS):
            nc.vector.quantize_mx(
                out=zero_g_codes[:, n * P : (n + 1) * P].bitcast(E5M2_X4),
                scales=zero_g_scales[:, n * P : (n + 1) * P],
                in_=zeros[:],
            )

        def warm_passes(count):
            for i in range(count):
                nc.tensor.matmul_mx(
                    out=gy_ps[PASSES - 1][:],
                    lhsT=zero_w_codes[:].bitcast(E4M3_X4),
                    lhsT_scale=zero_w_scales[:],
                    rhs=zero_g_codes[:].bitcast(E5M2_X4),
                    rhs_scale=zero_g_scales[:],
                    start=True,
                    stop=True,
                )

        warm_passes(WARM_FIRST)

        ident_f32 = sbuf.tile([P, P], F32)
        nc.vector.memset(ident_f32[:], 0.0)
        make_identity(nc, ident_f32[:], nomemset=True)
        ident_bf16 = sbuf.tile([P, P], BF16)
        nc.vector.memset(ident_bf16[:], 0.0)
        make_identity(nc, ident_bf16[:], nomemset=True)

        w_raw = sbuf.tile([P, PACK, FEATURES], BF16)
        nc.sync.dma_start(
            out=w_raw[:].rearrange("q (u e) i -> q u (e i)", u=2),
            in_=W_O.rearrange("(u q e) i -> q u (e i)", u=2, e=2),
        )
        g_raw = sbuf.tile([P, TOKEN_SETS * FEATURES], BF16)
        g_rows = grad_out.rearrange("b s o -> (b s) o").rearrange("(n p) o -> n p o", p=P)
        for n in range(TOKEN_SETS - 1):
            nc.sync.dma_start(out=g_raw[:, n * FEATURES : (n + 1) * FEATURES], in_=g_rows[n])
        last_set = TOKEN_SETS - 1
        for u in range(2):
            half = slice(u * FEATURES // 2, (u + 1) * FEATURES // 2)
            nc.sync.dma_start(
                out=g_raw[:, last_set * FEATURES + u * FEATURES // 2 : last_set * FEATURES + (u + 1) * FEATURES // 2],
                in_=g_rows[last_set][:, half],
            )
        kv_raw = sbuf.tile([P, BATCH, PACK, HEAD_DIM], BF16)
        nc.sync.dma_start(
            out=kv_raw[:].rearrange("p b r e -> p b (r e)"),
            in_=kv.rearrange("b h d e -> b (h d) e").rearrange("b (p r) e -> p b (r e)", r=PACK),
        )

        w_grouped = sbuf.tile([P, FEATURES, PACK], BF16, align_bytes=64)
        for copy, cols in ((nc.scalar.copy, slice(3 * P, 4 * P)), (nc.vector.tensor_copy, slice(0, 3 * P))):
            copy(
                out=w_grouped[:, cols, :].rearrange("q (c i) t -> q c t i", i=4),
                in_=w_raw[:, :, cols].rearrange("q t (c i) -> q c t i", i=4),
            )
        w_codes = sbuf.tile([P, FEATURES], U32, align_bytes=64)
        w_scales = sbuf.tile([P, FEATURES], U8, align_bytes=64)
        nc.vector.quantize_mx(
            out=w_codes[:].bitcast(E4M3_X4),
            scales=w_scales[:],
            in_=w_grouped[:].rearrange("q i t -> q (i t)"),
        )

        g_words = g_raw[:].bitcast(F32)
        g_grouped = sbuf.tile([P, TOKENS * PACK], BF16, align_bytes=64)
        g_grouped_words = g_grouped[:].bitcast(F32).rearrange("q (n p u) -> q n p u", n=TOKEN_SETS, u=2)
        g_codes = sbuf.tile([P, TOKENS], U32, align_bytes=64)
        g_scales = sbuf.tile([P, TOKENS], U8, align_bytes=64)
        words_per_token = FEATURES // 2
        for n in range(TOKEN_SETS):
            g_t = psum_work.tile([P, 2, P], F32, tag="work", name="g_t")
            for u in range(2):
                first = n * words_per_token + u * P
                nc.tensor.transpose(g_t[:, u, :], g_words[:, first : first + P], ident_f32[:])
            nc.scalar.copy(out=g_grouped_words[:, n, :, :], in_=g_t[:].rearrange("q u p -> q p u"))
            nc.vector.quantize_mx(
                out=g_codes[:, n * P : (n + 1) * P].bitcast(E5M2_X4),
                scales=g_scales[:, n * P : (n + 1) * P],
                in_=g_grouped[:, n * P * PACK : (n + 1) * P * PACK],
            )

        warm_passes(WARM_LAST)

        kv_t = sbuf.tile([P, HEADS, HEAD_DIM], F32)
        kv_ps = []
        for b in range(BATCH):
            kv_ps.append(psum_work.tile([P, PACK, P], BF16, tag="work", name="kv_ps%d" % b))
            for r in range(PACK):
                nc.tensor.transpose(kv_ps[b][:, r, :], kv_raw[:, b, r, :], ident_bf16[:])

        def kv_copy(copy, b):
            copy(
                out=kv_t[:, HEADS_PER_BATCH * b : HEADS_PER_BATCH * (b + 1), :].rearrange(
                    "e h (c r) -> e (h c) r", r=PACK
                ),
                in_=kv_ps[b][:].rearrange("e r p -> e p r"),
            )

        kv_copy(nc.scalar.copy, 0)

        for j in (0, 2, 1, 3):
            nc.tensor.matmul_mx(
                out=gy_ps[j][:],
                lhsT=w_codes[:, j * P : (j + 1) * P].bitcast(E4M3_X4),
                lhsT_scale=w_scales[:, j * P : (j + 1) * P],
                rhs=g_codes[:].bitcast(E5M2_X4),
                rhs_scale=g_scales[:],
                start=True,
                stop=True,
            )

        gy_sb = sbuf.tile([P, HEADS, 2, 2, HEAD_TOKENS], F32)
        for first, count in ((0, 2), (2, 2), (4, 4)):
            heads = slice(first, first + count)
            for jj in range(2):
                for jp in range(2):
                    copy = nc.scalar.copy if jp == 0 else nc.vector.tensor_copy
                    copy(
                        out=gy_sb[:, heads, jj, jp, :],
                        in_=gy_ps[2 * jp + jj][:].rearrange("e (h rr) -> e h rr", h=HEADS)[:, heads, :],
                    )
            if first == 2:
                kv_copy(nc.vector.tensor_copy, 1)

        out_rows = out.rearrange("b h (rr jp jj) d -> jp rr (b h) (jj d)", jp=2, jj=2)
        result = sbuf.tile([P, HEADS, 2 * HEAD_DIM], F32)
        for first_head in range(0, HEADS, 2):
            pair = (first_head, first_head + 1)
            last = first_head == HEADS - 2
            if last:
                halves = [
                    [psum_gy.tile([P, HEAD_DIM], F32, tag="gy", name="half_ps%d%d" % (k, jj)) for jj in range(2)]
                    for k in range(2)
                ]
            else:
                out_ps = [psum_work.tile([P, 2, HEAD_DIM], F32, tag="work", name="out_ps%d" % head) for head in pair]
                halves = [[out_ps[k][:, jj, :] for jj in range(2)] for k in range(2)]
            for jj in range(2):
                for k, head in enumerate(pair):
                    nc.tensor.matmul(
                        out=halves[k][jj][:] if last else halves[k][jj],
                        lhsT=gy_sb[:, head, jj, :, :].rearrange("e jp rr -> e (jp rr)"),
                        rhs=kv_t[:, head, :],
                        start=True,
                        stop=True,
                    )
                    if last:
                        copy = nc.scalar.copy if k == 0 else nc.vector.tensor_copy
                        copy(out=result[:, head, jj * HEAD_DIM : (jj + 1) * HEAD_DIM], in_=halves[k][jj][:])
            if not last:
                nc.vector.tensor_copy(out=result[:, pair[0], :], in_=out_ps[0][:].rearrange("s jj d -> s (jj d)"))
                nc.scalar.copy(out=result[:, pair[1], :], in_=out_ps[1][:].rearrange("s jj d -> s (jj d)"))
            for head in pair:
                for jp in range(2):
                    rows = slice(jp * HEAD_TOKENS, (jp + 1) * HEAD_TOKENS)
                    nc.sync.dma_start(out=out_rows[jp, :, head, :], in_=result[rows, head, :])
